import numpy as np
import ml_dtypes


def mxq(x, axis, fmt="e4m3"):
    dtype, down = {"e4m3": (ml_dtypes.float8_e4m3fn, 7), "e5m2": (ml_dtypes.float8_e5m2, 14)}[fmt]
    v = np.moveaxis(np.asarray(x, np.float32).astype(ml_dtypes.bfloat16).astype(np.float64), axis, -1)
    blocks = v.reshape(v.shape[:-1] + (-1, 32))
    amax = np.abs(blocks).max(-1, keepdims=True)
    byte = np.maximum(np.where(amax > 0, np.frexp(amax)[1] - 1 + 127, 0) - down, 1)
    scale = np.exp2(byte - 127.0)
    codes = (blocks / scale).astype(np.float32).astype(dtype).astype(np.float64)
    return np.moveaxis((codes * scale).reshape(v.shape), -1, axis)


WIDE = False


def mx_kscale(k):
    if not WIDE:
        return np.ones(k)
    levels = np.array([10, -10, 5, -5, 0])
    a = np.random.permutation(np.resize(levels, k // 512 * 4)).reshape(k // 512, 4)
    idx = np.arange(k)
    return np.exp2(a[idx // 512, idx % 128 // 32])


BF16 = ml_dtypes.bfloat16


def bf(x):
    return np.asarray(x, np.float32).astype(BF16)


def f64(x):
    return np.asarray(x).astype(np.float64)


L, N, E, H, C, LW, RW = 2048, 1, 1024, 8, 512, 1, 1
DH = E // H
W = L // C


def setup_inputs():
    t = mx_kscale(L)
    return {"q_scaled": bf(np.random.standard_normal((N * H, L, DH)) / np.sqrt(DH)),
            "k_heads": bf(np.random.standard_normal((N * H, L, DH)) * 0.5 * t[:, None]),
            "v_heads": bf(np.random.standard_normal((N * H, L, DH)) * 0.125 / t[:, None])}


def reference(q_scaled, k_heads, v_heads):
    q, k = f64(q_scaled), f64(k_heads)
    vq = mxq(f64(v_heads), 1, "e4m3")
    out = []
    for w in range(W):
        lo, hi = max(w - LW, 0) * C, min(w + RW + 1, W) * C
        dots = q[:, w * C:(w + 1) * C] @ k[:, lo:hi].transpose(0, 2, 1)
        attn = np.maximum(dots, 0.0)
        out.append(mxq(attn, 2, "e4m3") @ vq[:, lo:hi])
    return np.concatenate(out, axis=1)

@@ -1,0 +1,210 @@
+from contextlib import ExitStack
+
+import concourse.masks as masks
+import concourse.mybir as mybir
+
+BF16 = mybir.dt.bfloat16
+F32 = mybir.dt.float32
+U32 = mybir.dt.uint32
+U8 = mybir.dt.uint8
+FP8X4 = mybir.dt.float8_e4m3fn_x4
+RELU = mybir.ActivationFunctionType.Relu
+
+HEADS = 8
+TOKENS = 2048
+DH = 128
+P = 128
+PACK = 4
+CHUNK = P * PACK
+N_CHUNKS = TOKENS // CHUNK
+Q_TILES = CHUNK // P
+
+AHEAD = 2
+VECTOR_Q_TILE = 3
+
+DOTS_BANKS = 6
+
+FLOPS = 2 * 2 * HEADS * 10 * CHUNK * CHUNK * DH
+
+
+def seen_chunks(w):
+    return list(range(max(w - 1, 0), min(w + 2, N_CHUNKS)))
+
+
+def tile_normlocalattention_pa_kernel(tc, q_scaled, k_heads, v_heads, out):
+    nc = tc.nc
+
+    units = [(h, w) for h in range(HEADS) for w in range(N_CHUNKS)]
+    groups = []
+    first_group = []
+    for s, (h, w) in enumerate(units):
+        first_group.append(len(groups))
+        groups.extend((s, c) for c in seen_chunks(w))
+    unit_ending_at = {first_group[s] + len(seen_chunks(w)) - 1: s for s, (h, w) in enumerate(units)}
+
+    with ExitStack() as ctx:
+        const = ctx.enter_context(tc.tile_pool(name="const", bufs=1))
+        raw_pool = ctx.enter_context(tc.tile_pool(name="raw", bufs=3))
+        qk_pool = ctx.enter_context(tc.tile_pool(name="qk", bufs=AHEAD + 3))
+        v_pool = ctx.enter_context(tc.tile_pool(name="v", bufs=AHEAD + 4))
+        stage = ctx.enter_context(tc.tile_pool(name="stage", bufs=3))
+        attn_pool = ctx.enter_context(tc.tile_pool(name="attn", bufs=6))
+        dots_pool = ctx.enter_context(tc.psum_pool(name="dots", bufs=DOTS_BANKS))
+        flip_pool = ctx.enter_context(tc.psum_pool(name="flip", bufs=1))
+        sums_pool = ctx.enter_context(tc.psum_pool(name="sums", bufs=1))
+        ctx.enter_context(tc.manual_schedule())
+
+        raw = {}
+        flipped = {}
+        qk_t = {}
+        v_grouped = {}
+        v_words = {}
+        v_scales = {}
+        banks = {}
+        attn_grouped = {}
+        attn_words = {}
+        attn_scales = {}
+
+        identity = const.tile([P, P], BF16, name="identity")
+        masks.make_identity(nc, identity[:])
+
+        def load_head(h):
+            raw[h] = {
+                "q": raw_pool.tile([P, N_CHUNKS, PACK, DH], BF16, name="q_raw", tag="q_raw"),
+                "k": raw_pool.tile([P, N_CHUNKS, PACK, DH], BF16, name="k_raw", tag="k_raw"),
+                "v": raw_pool.tile([P, N_CHUNKS, PACK, DH], BF16, name="v_raw", tag="v_raw"),
+            }
+            for c in range(N_CHUNKS):
+                rows = slice(c * CHUNK, (c + 1) * CHUNK)
+                for name, source in (("q", q_scaled), ("k", k_heads), ("v", v_heads)):
+                    nc.sync.dma_start(
+                        out=raw[h][name][:, c],
+                        in_=source[h, rows, :].rearrange("(p j) d -> p j d", j=PACK),
+                    )
+
+        def transpose_plane(s, plane):
+            h, c = units[s]
+            if plane == 0:
+                flipped[s] = flip_pool.tile([P, 2 * PACK, P], BF16, name="flipped")
+            source = raw[h]["q" if plane < PACK else "k"]
+            nc.tensor.transpose(
+                out=flipped[s][:, plane, :], in_=source[:, c, plane % PACK, :], identity=identity[:]
+            )
+
+        def copy_transposes_out(s):
+            qk_t[s] = qk_pool.tile([P, 2 * PACK, P], BF16, name="qk_t")
+            nc.scalar.copy(out=qk_t[s][:], in_=flipped[s][:])
+
+        def group_v(s):
+            h, c = units[s]
+            v_grouped[s] = stage.tile([P, DH, PACK], BF16, name="v_grouped", align_bytes=64)
+            nc.vector.tensor_copy(
+                out=v_grouped[s][:], in_=raw[h]["v"][:, c].rearrange("p j d -> p d j")
+            )
+
+        def quantise_v(s):
+            v_words[s] = v_pool.tile([P, DH], U32, name="v_words", align_bytes=64)
+            v_scales[s] = v_pool.tile([P, DH], U8, name="v_scales", align_bytes=64)
+            nc.vector.quantize_mx(
+                out=v_words[s][:].bitcast(FP8X4),
+                scales=v_scales[s][:],
+                in_=v_grouped[s][:].rearrange("p d j -> p (d j)"),
+            )
+
+        def first_matmuls(g):
+            s, c = groups[g]
+            h, w = units[s]
+            keys = qk_t[h * N_CHUNKS + c]
+            weave = g == first_group[s] and s + AHEAD < len(units)
+            banks[g] = []
+            for t in range(Q_TILES):
+                bank = dots_pool.tile([P, PACK, P], F32, name="dots")
+                for j in range(PACK):
+                    nc.tensor.matmul(
+                        out=bank[:, j, :],
+                        lhsT=keys[:, PACK + j, :],
+                        rhs=qk_t[s][:, t, :],
+                        start=True,
+                        stop=True,
+                    )
+                    if weave and j % 2 == 0:
+                        transpose_plane(s + AHEAD, 2 * t + j // 2)
+                banks[g].append(bank)
+
+        def relu_out_of_psum(g):
+            attn_grouped[g] = stage.tile(
+                [P, Q_TILES, P, PACK], BF16, name="attn_grouped", align_bytes=64
+            )
+            for t in range(Q_TILES):
+                by_query = banks[g][t][:].rearrange("p j q -> p q j")
+                if t == VECTOR_Q_TILE:
+                    nc.vector.tensor_scalar_max(
+                        out=attn_grouped[g][:, t], in0=by_query, scalar1=0.0
+                    )
+                else:
+                    nc.scalar.activation(out=attn_grouped[g][:, t], in_=by_query, func=RELU)
+
+        def quantise_attn(g):
+            attn_words[g] = attn_pool.tile([P, CHUNK], U32, name="attn_words", align_bytes=64)
+            attn_scales[g] = attn_pool.tile([P, CHUNK], U8, name="attn_scales", align_bytes=64)
+            nc.vector.quantize_mx(
+                out=attn_words[g][:].bitcast(FP8X4),
+                scales=attn_scales[g][:],
+                in_=attn_grouped[g][:].rearrange("p t q j -> p (t q j)"),
+            )
+
+        def second_matmuls(s):
+            h, w = units[s]
+            sums = sums_pool.tile([P, Q_TILES, DH], F32, name="sums")
+            chunks = seen_chunks(w)
+            for t in range(Q_TILES):
+                queries = slice(t * P, (t + 1) * P)
+                for i, c in enumerate(chunks):
+                    g = first_group[s] + i
+                    nc.tensor.matmul_mx(
+                        out=sums[:, t, :],
+                        lhsT=attn_words[g][:, queries].bitcast(FP8X4),
+                        lhsT_scale=attn_scales[g][:, queries],
+                        rhs=v_words[h * N_CHUNKS + c][:].bitcast(FP8X4),
+                        rhs_scale=v_scales[h * N_CHUNKS + c][:],
+                        start=(i == 0),
+                        stop=(i == len(chunks) - 1),
+                    )
+            result = stage.tile([P, Q_TILES, DH], F32, name="result")
+            nc.vector.tensor_copy(out=result[:], in_=sums[:])
+            rows = slice(w * CHUNK, (w + 1) * CHUNK)
+            nc.sync.dma_start(
+                out=out[h, rows, :].rearrange("(p t) d -> p t d", t=Q_TILES), in_=result[:]
+            )
+
+        load_head(0)
+        load_head(1)
+        for s in range(AHEAD):
+            for plane in range(2 * PACK):
+                transpose_plane(s, plane)
+            copy_transposes_out(s)
+            group_v(s)
+        for s in range(AHEAD):
+            quantise_v(s)
+
+        for g in range(len(groups) + 2):
+            prepare = None
+            if g < len(groups):
+                s, c = groups[g]
+                h, w = units[s]
+                if g == first_group[s]:
+                    if w == 0 and h + 2 < HEADS:
+                        load_head(h + 2)
+                    if s + AHEAD < len(units):
+                        prepare = s + AHEAD
+                if prepare is not None:
+                    group_v(prepare)
+                first_matmuls(g)
+                relu_out_of_psum(g)
+            if 0 <= g - 1 < len(groups):
+                quantise_attn(g - 1)
+            if prepare is not None:
+                copy_transposes_out(prepare)
+                quantise_v(prepare)
+            if g - 2 in unit_ending_at:
+                second_matmuls(unit_ending_at[g - 2])

@@ -84,8 +84,6 @@ def tile_normlocalattention_pa_kernel(tc, q_scaled, k_heads, v_heads, out):
 
         def transpose_plane(s, plane):
             h, c = units[s]
-            if plane == 0:
-                flipped[s] = flip_pool.tile([P, 2 * PACK, P], BF16, name="flipped")
             source = raw[h]["q" if plane < PACK else "k"]
             nc.tensor.transpose(
                 out=flipped[s][:, plane, :], in_=source[:, c, plane % PACK, :], identity=identity[:]
@@ -93,7 +91,10 @@ def tile_normlocalattention_pa_kernel(tc, q_scaled, k_heads, v_heads, out):
 
         def copy_transposes_out(s):
             qk_t[s] = qk_pool.tile([P, 2 * PACK, P], BF16, name="qk_t")
-            nc.scalar.copy(out=qk_t[s][:], in_=flipped[s][:])
+            if s % 2 == 0:
+                nc.scalar.copy(out=qk_t[s][:], in_=flipped[s][:])
+            else:
+                nc.vector.tensor_copy(out=qk_t[s][:], in_=flipped[s][:])
 
         def group_v(s):
             h, c = units[s]
@@ -116,6 +117,8 @@ def tile_normlocalattention_pa_kernel(tc, q_scaled, k_heads, v_heads, out):
             h, w = units[s]
             keys = qk_t[h * N_CHUNKS + c]
             weave = g == first_group[s] and s + AHEAD < len(units)
+            if weave:
+                flipped[s + AHEAD] = flip_pool.tile([P, 2 * PACK, P], BF16, name="flipped")
             banks[g] = []
             for t in range(Q_TILES):
                 bank = dots_pool.tile([P, PACK, P], F32, name="dots")
@@ -155,7 +158,7 @@ def tile_normlocalattention_pa_kernel(tc, q_scaled, k_heads, v_heads, out):
 
         def second_matmuls(s):
             h, w = units[s]
-            sums = sums_pool.tile([P, Q_TILES, DH], F32, name="sums")
+            sums = sums_pool.tile([P, Q_TILES, DH], F32, name="sums", tag="sums")
             chunks = seen_chunks(w)
             for t in range(Q_TILES):
                 queries = slice(t * P, (t + 1) * P)
@@ -179,10 +182,14 @@ def tile_normlocalattention_pa_kernel(tc, q_scaled, k_heads, v_heads, out):
 
         load_head(0)
         load_head(1)
+        flipped[0] = flip_pool.tile([P, 2 * PACK, P], BF16, name="flipped")
+        flipped[1] = sums_pool.tile([P, 2 * PACK, P], BF16, name="borrowed", tag="sums")
         for s in range(AHEAD):
             for plane in range(2 * PACK):
                 transpose_plane(s, plane)
+        for s in range(AHEAD):
             copy_transposes_out(s)
+        for s in range(AHEAD):
             group_v(s)
         for s in range(AHEAD):
             quantise_v(s)

@@ -46,7 +46,7 @@ def tile_normlocalattention_pa_kernel(tc, q_scaled, k_heads, v_heads, out):
         const = ctx.enter_context(tc.tile_pool(name="const", bufs=1))
         raw_pool = ctx.enter_context(tc.tile_pool(name="raw", bufs=3))
         qk_pool = ctx.enter_context(tc.tile_pool(name="qk", bufs=AHEAD + 3))
-        v_pool = ctx.enter_context(tc.tile_pool(name="v", bufs=AHEAD + 4))
+        v_pool = ctx.enter_context(tc.tile_pool(name="v", bufs=2))
         stage = ctx.enter_context(tc.tile_pool(name="stage", bufs=3))
         attn_pool = ctx.enter_context(tc.tile_pool(name="attn", bufs=6))
         dots_pool = ctx.enter_context(tc.psum_pool(name="dots", bufs=DOTS_BANKS))
@@ -91,25 +91,27 @@ def tile_normlocalattention_pa_kernel(tc, q_scaled, k_heads, v_heads, out):
 
         def copy_transposes_out(s):
             qk_t[s] = qk_pool.tile([P, 2 * PACK, P], BF16, name="qk_t")
-            if s % 2 == 0:
+            if s % N_CHUNKS == 0:
                 nc.scalar.copy(out=qk_t[s][:], in_=flipped[s][:])
             else:
                 nc.vector.tensor_copy(out=qk_t[s][:], in_=flipped[s][:])
 
-        def group_v(s):
-            h, c = units[s]
-            v_grouped[s] = stage.tile([P, DH, PACK], BF16, name="v_grouped", align_bytes=64)
+        def group_v(h):
+            v_grouped[h] = v_pool.tile(
+                [P, N_CHUNKS, DH, PACK], BF16, name="v_grouped", align_bytes=64
+            )
             nc.vector.tensor_copy(
-                out=v_grouped[s][:], in_=raw[h]["v"][:, c].rearrange("p j d -> p d j")
+                out=v_grouped[h][:].rearrange("p c (e i) j -> p c e j i", i=4),
+                in_=raw[h]["v"][:].rearrange("p c j (e i) -> p c e j i", i=4),
             )
 
-        def quantise_v(s):
-            v_words[s] = v_pool.tile([P, DH], U32, name="v_words", align_bytes=64)
-            v_scales[s] = v_pool.tile([P, DH], U8, name="v_scales", align_bytes=64)
+        def quantise_v(h):
+            v_words[h] = v_pool.tile([P, N_CHUNKS, DH], U32, name="v_words", align_bytes=64)
+            v_scales[h] = v_pool.tile([P, N_CHUNKS, DH], U8, name="v_scales", align_bytes=64)
             nc.vector.quantize_mx(
-                out=v_words[s][:].bitcast(FP8X4),
-                scales=v_scales[s][:],
-                in_=v_grouped[s][:].rearrange("p d j -> p (d j)"),
+                out=v_words[h][:].rearrange("p c d -> p (c d)").bitcast(FP8X4),
+                scales=v_scales[h][:].rearrange("p c d -> p (c d)"),
+                in_=v_grouped[h][:].rearrange("p c d j -> p (c d j)"),
             )
 
         def first_matmuls(g):
@@ -168,8 +170,8 @@ def tile_normlocalattention_pa_kernel(tc, q_scaled, k_heads, v_heads, out):
                         out=sums[:, t, :],
                         lhsT=attn_words[g][:, queries].bitcast(FP8X4),
                         lhsT_scale=attn_scales[g][:, queries],
-                        rhs=v_words[h * N_CHUNKS + c][:].bitcast(FP8X4),
-                        rhs_scale=v_scales[h * N_CHUNKS + c][:],
+                        rhs=v_words[h][:, c, :].bitcast(FP8X4),
+                        rhs_scale=v_scales[h][:, c, :],
                         start=(i == 0),
                         stop=(i == len(chunks) - 1),
                     )
@@ -189,29 +191,26 @@ def tile_normlocalattention_pa_kernel(tc, q_scaled, k_heads, v_heads, out):
                 transpose_plane(s, plane)
         for s in range(AHEAD):
             copy_transposes_out(s)
-        for s in range(AHEAD):
-            group_v(s)
-        for s in range(AHEAD):
-            quantise_v(s)
+        group_v(0)
+        quantise_v(0)
 
         for g in range(len(groups) + 2):
-            prepare = None
             if g < len(groups):
                 s, c = groups[g]
                 h, w = units[s]
-                if g == first_group[s]:
-                    if w == 0 and h + 2 < HEADS:
-                        load_head(h + 2)
-                    if s + AHEAD < len(units):
-                        prepare = s + AHEAD
-                if prepare is not None:
-                    group_v(prepare)
+                if g == first_group[s] and w == 0 and h + 2 < HEADS:
+                    load_head(h + 2)
                 first_matmuls(g)
                 relu_out_of_psum(g)
             if 0 <= g - 1 < len(groups):
                 quantise_attn(g - 1)
-            if prepare is not None:
-                copy_transposes_out(prepare)
-                quantise_v(prepare)
+            if g < len(groups):
+                if g == first_group[s] and s + AHEAD < len(units):
+                    copy_transposes_out(s + AHEAD)
+                if g == first_group[s] + 2 and h + 1 < HEADS:
+                    if w == 1:
+                        group_v(h + 1)
+                    else:
+                        quantise_v(h + 1)
             if g - 2 in unit_ending_at:
                 second_matmuls(unit_ending_at[g - 2])

@@ -20,7 +20,7 @@ N_CHUNKS = TOKENS // CHUNK
 Q_TILES = CHUNK // P
 
 AHEAD = 2
-VECTOR_Q_TILE = 3
+VECTOR_Q_TILE = 1
 
 DOTS_BANKS = 6
 

@@ -9,6 +9,8 @@ U32 = mybir.dt.uint32
 U8 = mybir.dt.uint8
 FP8X4 = mybir.dt.float8_e4m3fn_x4
 RELU = mybir.ActivationFunctionType.Relu
+MULT = mybir.AluOpType.mult
+ADD = mybir.AluOpType.add
 
 HEADS = 8
 TOKENS = 2048
@@ -21,6 +23,8 @@ Q_TILES = CHUNK // P
 
 AHEAD = 2
 VECTOR_Q_TILE = 1
+
+V_PIECE = 64
 
 DOTS_BANKS = 6
 
@@ -91,7 +95,7 @@ def tile_normlocalattention_pa_kernel(tc, q_scaled, k_heads, v_heads, out):
 
         def copy_transposes_out(s):
             qk_t[s] = qk_pool.tile([P, 2 * PACK, P], BF16, name="qk_t")
-            if s % N_CHUNKS == 0:
+            if s == 0:
                 nc.scalar.copy(out=qk_t[s][:], in_=flipped[s][:])
             else:
                 nc.vector.tensor_copy(out=qk_t[s][:], in_=flipped[s][:])
@@ -100,10 +104,16 @@ def tile_normlocalattention_pa_kernel(tc, q_scaled, k_heads, v_heads, out):
             v_grouped[h] = v_pool.tile(
                 [P, N_CHUNKS, DH, PACK], BF16, name="v_grouped", align_bytes=64
             )
-            nc.vector.tensor_copy(
-                out=v_grouped[h][:].rearrange("p c (e i) j -> p c e j i", i=4),
-                in_=raw[h]["v"][:].rearrange("p c j (e i) -> p c e j i", i=4),
-            )
+            for c in range(N_CHUNKS):
+                for d0 in range(0, DH, V_PIECE):
+                    nc.gpsimd.tensor_scalar(
+                        out=v_grouped[h][:, c, d0 : d0 + V_PIECE, :],
+                        in0=raw[h]["v"][:, c, :, d0 : d0 + V_PIECE].rearrange("p j d -> p d j"),
+                        scalar1=1.0,
+                        scalar2=0.0,
+                        op0=MULT,
+                        op1=ADD,
+                    )
 
         def quantise_v(h):
             v_words[h] = v_pool.tile([P, N_CHUNKS, DH], U32, name="v_words", align_bytes=64)
@@ -192,7 +202,7 @@ def tile_normlocalattention_pa_kernel(tc, q_scaled, k_heads, v_heads, out):
         for s in range(AHEAD):
             copy_transposes_out(s)
         group_v(0)
-        quantise_v(0)
+        first_mx_step = min(unit_ending_at) + 2
 
         for g in range(len(groups) + 2):
             if g < len(groups):
@@ -200,6 +210,8 @@ def tile_normlocalattention_pa_kernel(tc, q_scaled, k_heads, v_heads, out):
                 h, w = units[s]
                 if g == first_group[s] and w == 0 and h + 2 < HEADS:
                     load_head(h + 2)
+                if g == first_group[s] and w == 0 and h + 1 < HEADS:
+                    group_v(h + 1)
                 first_matmuls(g)
                 relu_out_of_psum(g)
             if 0 <= g - 1 < len(groups):
@@ -207,10 +219,9 @@ def tile_normlocalattention_pa_kernel(tc, q_scaled, k_heads, v_heads, out):
             if g < len(groups):
                 if g == first_group[s] and s + AHEAD < len(units):
                     copy_transposes_out(s + AHEAD)
-                if g == first_group[s] + 2 and h + 1 < HEADS:
-                    if w == 1:
-                        group_v(h + 1)
-                    else:
-                        quantise_v(h + 1)
+                if g == first_group[s] + 2 and w == 2 and h + 1 < HEADS:
+                    quantise_v(h + 1)
+                if g == first_mx_step - 1:
+                    quantise_v(0)
             if g - 2 in unit_ending_at:
                 second_matmuls(unit_ending_at[g - 2])

@@ -23,8 +23,16 @@ Q_TILES = CHUNK // P
 
 AHEAD = 2
 VECTOR_Q_TILE = 1
+SPARE_Q_TILE = 3
 
 V_PIECE = 64
+
+LOAD_ORDER = (
+    [("q", 0), ("k", 0), ("k", 1), ("q", 1), ("q", 2), ("k", 2)]
+    + [("v", c) for c in range(N_CHUNKS)]
+    + [("q", 3), ("k", 3)]
+)
+WARM_UP = 16
 
 DOTS_BANKS = 6
 
@@ -52,6 +60,7 @@ def tile_normlocalattention_pa_kernel(tc, q_scaled, k_heads, v_heads, out):
         qk_pool = ctx.enter_context(tc.tile_pool(name="qk", bufs=AHEAD + 3))
         v_pool = ctx.enter_context(tc.tile_pool(name="v", bufs=2))
         stage = ctx.enter_context(tc.tile_pool(name="stage", bufs=3))
+        result_pool = ctx.enter_context(tc.tile_pool(name="result", bufs=5))
         attn_pool = ctx.enter_context(tc.tile_pool(name="attn", bufs=6))
         dots_pool = ctx.enter_context(tc.psum_pool(name="dots", bufs=DOTS_BANKS))
         flip_pool = ctx.enter_context(tc.psum_pool(name="flip", bufs=1))
@@ -78,13 +87,13 @@ def tile_normlocalattention_pa_kernel(tc, q_scaled, k_heads, v_heads, out):
                 "k": raw_pool.tile([P, N_CHUNKS, PACK, DH], BF16, name="k_raw", tag="k_raw"),
                 "v": raw_pool.tile([P, N_CHUNKS, PACK, DH], BF16, name="v_raw", tag="v_raw"),
             }
-            for c in range(N_CHUNKS):
+            sources = {"q": q_scaled, "k": k_heads, "v": v_heads}
+            for name, c in LOAD_ORDER:
                 rows = slice(c * CHUNK, (c + 1) * CHUNK)
-                for name, source in (("q", q_scaled), ("k", k_heads), ("v", v_heads)):
-                    nc.sync.dma_start(
-                        out=raw[h][name][:, c],
-                        in_=source[h, rows, :].rearrange("(p j) d -> p j d", j=PACK),
-                    )
+                nc.sync.dma_start(
+                    out=raw[h][name][:, c],
+                    in_=sources[name][h, rows, :].rearrange("(p j) d -> p j d", j=PACK),
+                )
 
         def transpose_plane(s, plane):
             h, c = units[s]
@@ -95,10 +104,7 @@ def tile_normlocalattention_pa_kernel(tc, q_scaled, k_heads, v_heads, out):
 
         def copy_transposes_out(s):
             qk_t[s] = qk_pool.tile([P, 2 * PACK, P], BF16, name="qk_t")
-            if s == 0:
-                nc.scalar.copy(out=qk_t[s][:], in_=flipped[s][:])
-            else:
-                nc.vector.tensor_copy(out=qk_t[s][:], in_=flipped[s][:])
+            nc.vector.tensor_copy(out=qk_t[s][:], in_=flipped[s][:])
 
         def group_v(h):
             v_grouped[h] = v_pool.tile(
@@ -146,38 +152,41 @@ def tile_normlocalattention_pa_kernel(tc, q_scaled, k_heads, v_heads, out):
                         transpose_plane(s + AHEAD, 2 * t + j // 2)
                 banks[g].append(bank)
 
-        def relu_out_of_psum(g):
+        def relu_out_of_psum(g, vector_tiles):
             attn_grouped[g] = stage.tile(
                 [P, Q_TILES, P, PACK], BF16, name="attn_grouped", align_bytes=64
             )
             for t in range(Q_TILES):
                 by_query = banks[g][t][:].rearrange("p j q -> p q j")
-                if t == VECTOR_Q_TILE:
+                if t in vector_tiles:
                     nc.vector.tensor_scalar_max(
                         out=attn_grouped[g][:, t], in0=by_query, scalar1=0.0
                     )
                 else:
                     nc.scalar.activation(out=attn_grouped[g][:, t], in_=by_query, func=RELU)
 
-        def quantise_attn(g):
+        def quantise_attn(g, pieces):
             attn_words[g] = attn_pool.tile([P, CHUNK], U32, name="attn_words", align_bytes=64)
             attn_scales[g] = attn_pool.tile([P, CHUNK], U8, name="attn_scales", align_bytes=64)
-            nc.vector.quantize_mx(
-                out=attn_words[g][:].bitcast(FP8X4),
-                scales=attn_scales[g][:],
-                in_=attn_grouped[g][:].rearrange("p t q j -> p (t q j)"),
-            )
+            width = CHUNK // pieces
+            for n in range(pieces):
+                nc.vector.quantize_mx(
+                    out=attn_words[g][:, n * width : (n + 1) * width].bitcast(FP8X4),
+                    scales=attn_scales[g][:, n * width : (n + 1) * width],
+                    in_=attn_grouped[g][:].rearrange("p t q j -> p (t q j)")[
+                        :, n * width * PACK : (n + 1) * width * PACK
+                    ],
+                )
 
-        def second_matmuls(s):
+        def second_matmuls(s, tiles, sums, copy_out):
             h, w = units[s]
-            sums = sums_pool.tile([P, Q_TILES, DH], F32, name="sums", tag="sums")
             chunks = seen_chunks(w)
-            for t in range(Q_TILES):
+            for n, t in enumerate(tiles):
                 queries = slice(t * P, (t + 1) * P)
                 for i, c in enumerate(chunks):
                     g = first_group[s] + i
                     nc.tensor.matmul_mx(
-                        out=sums[:, t, :],
+                        out=sums[:, n, :],
                         lhsT=attn_words[g][:, queries].bitcast(FP8X4),
                         lhsT_scale=attn_scales[g][:, queries],
                         rhs=v_words[h][:, c, :].bitcast(FP8X4),
@@ -185,43 +194,77 @@ def tile_normlocalattention_pa_kernel(tc, q_scaled, k_heads, v_heads, out):
                         start=(i == 0),
                         stop=(i == len(chunks) - 1),
                     )
-            result = stage.tile([P, Q_TILES, DH], F32, name="result")
-            nc.vector.tensor_copy(out=result[:], in_=sums[:])
+            result = result_pool.tile([P, len(tiles), DH], F32, name="result")
+            copy_out(out=result[:], in_=sums[:])
             rows = slice(w * CHUNK, (w + 1) * CHUNK)
             nc.sync.dma_start(
-                out=out[h, rows, :].rearrange("(p t) d -> p t d", t=Q_TILES), in_=result[:]
+                out=out[h, rows, :].rearrange("(p t) d -> p t d", t=Q_TILES)[
+                    :, tiles[0] : tiles[-1] + 1, :
+                ],
+                in_=result[:],
             )
+
+        def whole_unit(s, copy_out):
+            sums = sums_pool.tile([P, Q_TILES, DH], F32, name="sums", tag="sums")
+            second_matmuls(s, list(range(Q_TILES)), sums, copy_out)
 
         load_head(0)
         load_head(1)
-        flipped[0] = flip_pool.tile([P, 2 * PACK, P], BF16, name="flipped")
-        flipped[1] = sums_pool.tile([P, 2 * PACK, P], BF16, name="borrowed", tag="sums")
+        zeros = const.tile([P, P], BF16, name="zeros")
+        nc.vector.memset(zeros[:], 0.0)
+        unread = dots_pool.tile([P, PACK, P], F32, name="dots")
+        for i in range(WARM_UP):
+            nc.tensor.matmul(
+                out=unread[:, i % PACK, :], lhsT=zeros[:], rhs=zeros[:], start=True, stop=True
+            )
+        halves = [(s, first) for s in range(AHEAD) for first in (PACK, 0)]
+        for s, first in halves:
+            flipped[s, first] = dots_pool.tile([P, PACK, P], BF16, name="dots")
+            h, c = units[s]
+            for j in range(PACK):
+                nc.tensor.transpose(
+                    out=flipped[s, first][:, j, :],
+                    in_=raw[h]["k" if first else "q"][:, c, j, :],
+                    identity=identity[:],
+                )
         for s in range(AHEAD):
-            for plane in range(2 * PACK):
-                transpose_plane(s, plane)
-        for s in range(AHEAD):
-            copy_transposes_out(s)
+            qk_t[s] = qk_pool.tile([P, 2 * PACK, P], BF16, name="qk_t")
+        for s, first in halves:
+            planes = qk_t[s][:, first : first + PACK, :]
+            if first:
+                nc.scalar.copy(out=planes, in_=flipped[s, first][:])
+            else:
+                nc.vector.tensor_copy(out=planes, in_=flipped[s, first][:])
         group_v(0)
         first_mx_step = min(unit_ending_at) + 2
 
-        for g in range(len(groups) + 2):
-            if g < len(groups):
-                s, c = groups[g]
-                h, w = units[s]
-                if g == first_group[s] and w == 0 and h + 2 < HEADS:
-                    load_head(h + 2)
-                if g == first_group[s] and w == 0 and h + 1 < HEADS:
-                    group_v(h + 1)
-                first_matmuls(g)
-                relu_out_of_psum(g)
-            if 0 <= g - 1 < len(groups):
-                quantise_attn(g - 1)
-            if g < len(groups):
-                if g == first_group[s] and s + AHEAD < len(units):
-                    copy_transposes_out(s + AHEAD)
-                if g == first_group[s] + 2 and w == 2 and h + 1 < HEADS:
-                    quantise_v(h + 1)
-                if g == first_mx_step - 1:
-                    quantise_v(0)
+        last = len(groups) - 1
+        for g in range(last):
+            s, c = groups[g]
+            h, w = units[s]
+            if g == first_group[s] and w == 0 and h + 2 < HEADS:
+                load_head(h + 2)
+            if g == first_group[s] and w == 0 and h + 1 < HEADS:
+                group_v(h + 1)
+            first_matmuls(g)
+            spare = g == first_group[s] and s + AHEAD >= len(units)
+            relu_out_of_psum(g, (VECTOR_Q_TILE, SPARE_Q_TILE) if spare else (VECTOR_Q_TILE,))
+            if g >= 1:
+                quantise_attn(g - 1, 1)
+            if g == first_group[s] and s + AHEAD < len(units):
+                copy_transposes_out(s + AHEAD)
+            if g == first_group[s] + 2 and w == 2 and h + 1 < HEADS:
+                quantise_v(h + 1)
+            if g == first_mx_step - 1:
+                quantise_v(0)
             if g - 2 in unit_ending_at:
-                second_matmuls(unit_ending_at[g - 2])
+                whole_unit(unit_ending_at[g - 2], nc.vector.tensor_copy)
+
+        first_matmuls(last)
+        relu_out_of_psum(last, ())
+        quantise_attn(last - 1, 1)
+        whole_unit(unit_ending_at[last - 2], nc.scalar.copy)
+        quantise_attn(last, Q_TILES)
+        for t in range(Q_TILES):
+            tile_sums = dots_pool.tile([P, 1, DH], F32, name="dots")
+            second_matmuls(len(units) - 1, [t], tile_sums, nc.vector.tensor_copy)

@@ -23,6 +23,7 @@ Q_TILES = CHUNK // P
 
 AHEAD = 2
 VECTOR_Q_TILE = 1
+SCALAR_SUMS_EVERY = 8
 SPARE_Q_TILE = 3
 
 V_PIECE = 64
@@ -59,9 +60,9 @@ def tile_normlocalattention_pa_kernel(tc, q_scaled, k_heads, v_heads, out):
         raw_pool = ctx.enter_context(tc.tile_pool(name="raw", bufs=3))
         qk_pool = ctx.enter_context(tc.tile_pool(name="qk", bufs=AHEAD + 3))
         v_pool = ctx.enter_context(tc.tile_pool(name="v", bufs=2))
-        stage = ctx.enter_context(tc.tile_pool(name="stage", bufs=3))
+        stage = ctx.enter_context(tc.tile_pool(name="stage", bufs=5))
         result_pool = ctx.enter_context(tc.tile_pool(name="result", bufs=5))
-        attn_pool = ctx.enter_context(tc.tile_pool(name="attn", bufs=6))
+        attn_pool = ctx.enter_context(tc.tile_pool(name="attn", bufs=9))
         dots_pool = ctx.enter_context(tc.psum_pool(name="dots", bufs=DOTS_BANKS))
         flip_pool = ctx.enter_context(tc.psum_pool(name="flip", bufs=1))
         sums_pool = ctx.enter_context(tc.psum_pool(name="sums", bufs=1))
@@ -258,10 +259,12 @@ def tile_normlocalattention_pa_kernel(tc, q_scaled, k_heads, v_heads, out):
             if g == first_mx_step - 1:
                 quantise_v(0)
             if g - 2 in unit_ending_at:
-                whole_unit(unit_ending_at[g - 2], nc.vector.tensor_copy)
+                done = unit_ending_at[g - 2]
+                by_scalar = done % SCALAR_SUMS_EVERY == 0
+                whole_unit(done, nc.scalar.copy if by_scalar else nc.vector.tensor_copy)
 
         first_matmuls(last)
-        relu_out_of_psum(last, ())
+        relu_out_of_psum(last, (VECTOR_Q_TILE,))
         quantise_attn(last - 1, 1)
         whole_unit(unit_ending_at[last - 2], nc.scalar.copy)
         quantise_attn(last, Q_TILES)

@@ -23,7 +23,6 @@ Q_TILES = CHUNK // P
 
 AHEAD = 2
 VECTOR_Q_TILE = 1
-SCALAR_SUMS_EVERY = 8
 SPARE_Q_TILE = 3
 
 V_PIECE = 64
@@ -259,9 +258,7 @@ def tile_normlocalattention_pa_kernel(tc, q_scaled, k_heads, v_heads, out):
             if g == first_mx_step - 1:
                 quantise_v(0)
             if g - 2 in unit_ending_at:
-                done = unit_ending_at[g - 2]
-                by_scalar = done % SCALAR_SUMS_EVERY == 0
-                whole_unit(done, nc.scalar.copy if by_scalar else nc.vector.tensor_copy)
+                whole_unit(unit_ending_at[g - 2], nc.vector.tensor_copy)
 
         first_matmuls(last)
         relu_out_of_psum(last, (VECTOR_Q_TILE,))

@@ -34,6 +34,8 @@ LOAD_ORDER = (
 )
 WARM_UP = 16
 
+BORROWING_GROUP = 1
+
 DOTS_BANKS = 6
 
 FLOPS = 2 * 2 * HEADS * 10 * CHUNK * CHUNK * DH
@@ -53,6 +55,10 @@ def tile_normlocalattention_pa_kernel(tc, q_scaled, k_heads, v_heads, out):
         first_group.append(len(groups))
         groups.extend((s, c) for c in seen_chunks(w))
     unit_ending_at = {first_group[s] + len(seen_chunks(w)) - 1: s for s, (h, w) in enumerate(units)}
+    all_planes = list(range(2 * PACK))
+    woven_in = {first_group[s]: (s + AHEAD, all_planes) for s in range(1, len(units) - AHEAD)}
+    woven_in[0] = (1, all_planes[:PACK])
+    woven_in[1] = (2, all_planes)
 
     with ExitStack() as ctx:
         const = ctx.enter_context(tc.tile_pool(name="const", bufs=1))
@@ -102,9 +108,11 @@ def tile_normlocalattention_pa_kernel(tc, q_scaled, k_heads, v_heads, out):
                 out=flipped[s][:, plane, :], in_=source[:, c, plane % PACK, :], identity=identity[:]
             )
 
-        def copy_transposes_out(s):
-            qk_t[s] = qk_pool.tile([P, 2 * PACK, P], BF16, name="qk_t")
-            nc.vector.tensor_copy(out=qk_t[s][:], in_=flipped[s][:])
+        def copy_transposes_out(s, planes):
+            if s not in qk_t:
+                qk_t[s] = qk_pool.tile([P, 2 * PACK, P], BF16, name="qk_t")
+            run = slice(planes[0], planes[-1] + 1)
+            nc.vector.tensor_copy(out=qk_t[s][:, run], in_=flipped[s][:, run])
 
         def group_v(h):
             v_grouped[h] = v_pool.tile(
@@ -121,22 +129,27 @@ def tile_normlocalattention_pa_kernel(tc, q_scaled, k_heads, v_heads, out):
                         op1=ADD,
                     )
 
-        def quantise_v(h):
-            v_words[h] = v_pool.tile([P, N_CHUNKS, DH], U32, name="v_words", align_bytes=64)
-            v_scales[h] = v_pool.tile([P, N_CHUNKS, DH], U8, name="v_scales", align_bytes=64)
+        def quantise_v(h, chunks):
+            if chunks[0] == 0:
+                v_words[h] = v_pool.tile([P, N_CHUNKS, DH], U32, name="v_words", align_bytes=64)
+                v_scales[h] = v_pool.tile([P, N_CHUNKS, DH], U8, name="v_scales", align_bytes=64)
+            run = slice(chunks[0], chunks[-1] + 1)
             nc.vector.quantize_mx(
-                out=v_words[h][:].rearrange("p c d -> p (c d)").bitcast(FP8X4),
-                scales=v_scales[h][:].rearrange("p c d -> p (c d)"),
-                in_=v_grouped[h][:].rearrange("p c d j -> p (c d j)"),
+                out=v_words[h][:, run].rearrange("p c d -> p (c d)").bitcast(FP8X4),
+                scales=v_scales[h][:, run].rearrange("p c d -> p (c d)"),
+                in_=v_grouped[h][:, run].rearrange("p c d j -> p (c d j)"),
             )
 
         def first_matmuls(g):
             s, c = groups[g]
             h, w = units[s]
             keys = qk_t[h * N_CHUNKS + c]
-            weave = g == first_group[s] and s + AHEAD < len(units)
-            if weave:
-                flipped[s + AHEAD] = flip_pool.tile([P, 2 * PACK, P], BF16, name="flipped")
+            ahead, planes = woven_in.get(g, (None, []))
+            if planes and g == BORROWING_GROUP:
+                flipped[ahead] = sums_pool.tile([P, 2 * PACK, P], BF16, name="borrowed", tag="sums")
+            elif planes:
+                flipped[ahead] = flip_pool.tile([P, 2 * PACK, P], BF16, name="flipped")
+            places = 2 * Q_TILES
             banks[g] = []
             for t in range(Q_TILES):
                 bank = dots_pool.tile([P, PACK, P], F32, name="dots")
@@ -148,8 +161,9 @@ def tile_normlocalattention_pa_kernel(tc, q_scaled, k_heads, v_heads, out):
                         start=True,
                         stop=True,
                     )
-                    if weave and j % 2 == 0:
-                        transpose_plane(s + AHEAD, 2 * t + j // 2)
+                    place = 2 * t + j // 2
+                    if j % 2 == 0 and place >= places - len(planes):
+                        transpose_plane(ahead, planes[place - (places - len(planes))])
                 banks[g].append(bank)
 
         def relu_out_of_psum(g, vector_tiles):
@@ -217,13 +231,14 @@ def tile_normlocalattention_pa_kernel(tc, q_scaled, k_heads, v_heads, out):
             nc.tensor.matmul(
                 out=unread[:, i % PACK, :], lhsT=zeros[:], rhs=zeros[:], start=True, stop=True
             )
-        halves = [(s, first) for s in range(AHEAD) for first in (PACK, 0)]
+        early = {}
+        halves = [(0, PACK), (0, 0), (1, PACK)]
         for s, first in halves:
-            flipped[s, first] = dots_pool.tile([P, PACK, P], BF16, name="dots")
+            early[s, first] = dots_pool.tile([P, PACK, P], BF16, name="dots")
             h, c = units[s]
             for j in range(PACK):
                 nc.tensor.transpose(
-                    out=flipped[s, first][:, j, :],
+                    out=early[s, first][:, j, :],
                     in_=raw[h]["k" if first else "q"][:, c, j, :],
                     identity=identity[:],
                 )
@@ -232,9 +247,9 @@ def tile_normlocalattention_pa_kernel(tc, q_scaled, k_heads, v_heads, out):
         for s, first in halves:
             planes = qk_t[s][:, first : first + PACK, :]
             if first:
-                nc.scalar.copy(out=planes, in_=flipped[s, first][:])
+                nc.scalar.copy(out=planes, in_=early[s, first][:])
             else:
-                nc.vector.tensor_copy(out=planes, in_=flipped[s, first][:])
+                nc.vector.tensor_copy(out=planes, in_=early[s, first][:])
         group_v(0)
         first_mx_step = min(unit_ending_at) + 2
 
@@ -247,16 +262,18 @@ def tile_normlocalattention_pa_kernel(tc, q_scaled, k_heads, v_heads, out):
             if g == first_group[s] and w == 0 and h + 1 < HEADS:
                 group_v(h + 1)
             first_matmuls(g)
-            spare = g == first_group[s] and s + AHEAD >= len(units)
+            spare = g == first_group[s] and g not in woven_in
             relu_out_of_psum(g, (VECTOR_Q_TILE, SPARE_Q_TILE) if spare else (VECTOR_Q_TILE,))
             if g >= 1:
                 quantise_attn(g - 1, 1)
-            if g == first_group[s] and s + AHEAD < len(units):
-                copy_transposes_out(s + AHEAD)
+            if g in woven_in:
+                copy_transposes_out(woven_in[g][0], woven_in[g][1])
             if g == first_group[s] + 2 and w == 2 and h + 1 < HEADS:
-                quantise_v(h + 1)
+                quantise_v(h + 1, [0, 1, 2, 3])
             if g == first_mx_step - 1:
-                quantise_v(0)
+                quantise_v(0, [0, 1])
+            if g == first_group[1] + 2:
+                quantise_v(0, [2, 3])
             if g - 2 in unit_ending_at:
                 whole_unit(unit_ending_at[g - 2], nc.vector.tensor_copy)
 

@@ -26,6 +26,7 @@ VECTOR_Q_TILE = 1
 SPARE_Q_TILE = 3
 
 V_PIECE = 64
+PIECE_LAG = 4
 
 LOAD_ORDER = (
     [("q", 0), ("k", 0), ("k", 1), ("q", 1), ("q", 2), ("k", 2)]
@@ -59,12 +60,18 @@ def tile_normlocalattention_pa_kernel(tc, q_scaled, k_heads, v_heads, out):
     woven_in = {first_group[s]: (s + AHEAD, all_planes) for s in range(1, len(units) - AHEAD)}
     woven_in[0] = (1, all_planes[:PACK])
     woven_in[1] = (2, all_planes)
+    v_pieces = [
+        (h, c, d0) for h in range(1, HEADS) for c in range(N_CHUNKS) for d0 in range(0, DH, V_PIECE)
+    ]
+    copy_steps = [g for g in range(len(groups) - 1) if g in woven_in or g - 2 in unit_ending_at]
+    piece_at = {copy_steps[n + PIECE_LAG]: n for n in range(len(v_pieces))}
 
     with ExitStack() as ctx:
         const = ctx.enter_context(tc.tile_pool(name="const", bufs=1))
         raw_pool = ctx.enter_context(tc.tile_pool(name="raw", bufs=3))
         qk_pool = ctx.enter_context(tc.tile_pool(name="qk", bufs=AHEAD + 3))
         v_pool = ctx.enter_context(tc.tile_pool(name="v", bufs=2))
+        piece_pool = ctx.enter_context(tc.tile_pool(name="piece", bufs=1))
         stage = ctx.enter_context(tc.tile_pool(name="stage", bufs=5))
         result_pool = ctx.enter_context(tc.tile_pool(name="result", bufs=5))
         attn_pool = ctx.enter_context(tc.tile_pool(name="attn", bufs=9))
@@ -77,6 +84,7 @@ def tile_normlocalattention_pa_kernel(tc, q_scaled, k_heads, v_heads, out):
         flipped = {}
         qk_t = {}
         v_grouped = {}
+        v_piece = {}
         v_words = {}
         v_scales = {}
         banks = {}
@@ -128,6 +136,29 @@ def tile_normlocalattention_pa_kernel(tc, q_scaled, k_heads, v_heads, out):
                         op0=MULT,
                         op1=ADD,
                     )
+
+        def group_v_piece(n):
+            h, c, d0 = v_pieces[n]
+            v_piece[n] = piece_pool.tile([P, V_PIECE, PACK], BF16, name="v_piece", align_bytes=64)
+            nc.gpsimd.tensor_scalar(
+                out=v_piece[n][:],
+                in0=raw[h]["v"][:, c, :, d0 : d0 + V_PIECE].rearrange("p j d -> p d j"),
+                scalar1=1.0,
+                scalar2=0.0,
+                op0=MULT,
+                op1=ADD,
+            )
+
+        def quantise_v_piece(n):
+            h, c, d0 = v_pieces[n]
+            if (c, d0) == (0, 0):
+                v_words[h] = v_pool.tile([P, N_CHUNKS, DH], U32, name="v_words", align_bytes=64)
+                v_scales[h] = v_pool.tile([P, N_CHUNKS, DH], U8, name="v_scales", align_bytes=64)
+            nc.vector.quantize_mx(
+                out=v_words[h][:, c, d0 : d0 + V_PIECE].bitcast(FP8X4),
+                scales=v_scales[h][:, c, d0 : d0 + V_PIECE],
+                in_=v_piece[n][:].rearrange("p d j -> p (d j)"),
+            )
 
         def quantise_v(h, chunks):
             if chunks[0] == 0:
@@ -251,6 +282,7 @@ def tile_normlocalattention_pa_kernel(tc, q_scaled, k_heads, v_heads, out):
             else:
                 nc.vector.tensor_copy(out=planes, in_=early[s, first][:])
         group_v(0)
+        group_v_piece(0)
         first_mx_step = min(unit_ending_at) + 2
 
         last = len(groups) - 1
@@ -259,17 +291,17 @@ def tile_normlocalattention_pa_kernel(tc, q_scaled, k_heads, v_heads, out):
             h, w = units[s]
             if g == first_group[s] and w == 0 and h + 2 < HEADS:
                 load_head(h + 2)
-            if g == first_group[s] and w == 0 and h + 1 < HEADS:
-                group_v(h + 1)
             first_matmuls(g)
             spare = g == first_group[s] and g not in woven_in
             relu_out_of_psum(g, (VECTOR_Q_TILE, SPARE_Q_TILE) if spare else (VECTOR_Q_TILE,))
             if g >= 1:
                 quantise_attn(g - 1, 1)
+            if g in piece_at:
+                quantise_v_piece(piece_at[g])
+                if piece_at[g] + 1 < len(v_pieces):
+                    group_v_piece(piece_at[g] + 1)
             if g in woven_in:
                 copy_transposes_out(woven_in[g][0], woven_in[g][1])
-            if g == first_group[s] + 2 and w == 2 and h + 1 < HEADS:
-                quantise_v(h + 1, [0, 1, 2, 3])
             if g == first_mx_step - 1:
                 quantise_v(0, [0, 1])
             if g == first_group[1] + 2:

@@ -25,8 +25,7 @@ AHEAD = 2
 VECTOR_Q_TILE = 1
 SPARE_Q_TILE = 3
 
-V_PIECE = 64
-PIECE_LAG = 4
+V_LAG = 1
 
 LOAD_ORDER = (
     [("q", 0), ("k", 0), ("k", 1), ("q", 1), ("q", 2), ("k", 2)]
@@ -60,11 +59,9 @@ def tile_normlocalattention_pa_kernel(tc, q_scaled, k_heads, v_heads, out):
     woven_in = {first_group[s]: (s + AHEAD, all_planes) for s in range(1, len(units) - AHEAD)}
     woven_in[0] = (1, all_planes[:PACK])
     woven_in[1] = (2, all_planes)
-    v_pieces = [
-        (h, c, d0) for h in range(1, HEADS) for c in range(N_CHUNKS) for d0 in range(0, DH, V_PIECE)
-    ]
-    copy_steps = [g for g in range(len(groups) - 1) if g in woven_in or g - 2 in unit_ending_at]
-    piece_at = {copy_steps[n + PIECE_LAG]: n for n in range(len(v_pieces))}
+    v_pieces = [(h, c) for h in range(1, HEADS) for c in range(N_CHUNKS)]
+    sums_steps = [g for g in range(len(groups) - 1) if g - 2 in unit_ending_at]
+    piece_at = {sums_steps[n + V_LAG]: n for n in range(len(v_pieces))}
 
     with ExitStack() as ctx:
         const = ctx.enter_context(tc.tile_pool(name="const", bufs=1))
@@ -127,22 +124,21 @@ def tile_normlocalattention_pa_kernel(tc, q_scaled, k_heads, v_heads, out):
                 [P, N_CHUNKS, DH, PACK], BF16, name="v_grouped", align_bytes=64
             )
             for c in range(N_CHUNKS):
-                for d0 in range(0, DH, V_PIECE):
-                    nc.gpsimd.tensor_scalar(
-                        out=v_grouped[h][:, c, d0 : d0 + V_PIECE, :],
-                        in0=raw[h]["v"][:, c, :, d0 : d0 + V_PIECE].rearrange("p j d -> p d j"),
-                        scalar1=1.0,
-                        scalar2=0.0,
-                        op0=MULT,
-                        op1=ADD,
-                    )
+                nc.gpsimd.tensor_scalar(
+                    out=v_grouped[h][:, c],
+                    in0=raw[h]["v"][:, c].rearrange("p j d -> p d j"),
+                    scalar1=1.0,
+                    scalar2=0.0,
+                    op0=MULT,
+                    op1=ADD,
+                )
 
         def group_v_piece(n):
-            h, c, d0 = v_pieces[n]
-            v_piece[n] = piece_pool.tile([P, V_PIECE, PACK], BF16, name="v_piece", align_bytes=64)
+            h, c = v_pieces[n]
+            v_piece[n] = piece_pool.tile([P, DH, PACK], BF16, name="v_piece", align_bytes=64)
             nc.gpsimd.tensor_scalar(
                 out=v_piece[n][:],
-                in0=raw[h]["v"][:, c, :, d0 : d0 + V_PIECE].rearrange("p j d -> p d j"),
+                in0=raw[h]["v"][:, c].rearrange("p j d -> p d j"),
                 scalar1=1.0,
                 scalar2=0.0,
                 op0=MULT,
@@ -150,13 +146,13 @@ def tile_normlocalattention_pa_kernel(tc, q_scaled, k_heads, v_heads, out):
             )
 
         def quantise_v_piece(n):
-            h, c, d0 = v_pieces[n]
-            if (c, d0) == (0, 0):
+            h, c = v_pieces[n]
+            if c == 0:
                 v_words[h] = v_pool.tile([P, N_CHUNKS, DH], U32, name="v_words", align_bytes=64)
                 v_scales[h] = v_pool.tile([P, N_CHUNKS, DH], U8, name="v_scales", align_bytes=64)
             nc.vector.quantize_mx(
-                out=v_words[h][:, c, d0 : d0 + V_PIECE].bitcast(FP8X4),
-                scales=v_scales[h][:, c, d0 : d0 + V_PIECE],
+                out=v_words[h][:, c].bitcast(FP8X4),
+                scales=v_scales[h][:, c],
                 in_=v_piece[n][:].rearrange("p d j -> p (d j)"),
             )
 

@@ -25,7 +25,8 @@ AHEAD = 2
 VECTOR_Q_TILE = 1
 SPARE_Q_TILE = 3
 
-V_LAG = 1
+FIRST_V_STEPS = [1, 2]
+MX_LAG = 2
 
 LOAD_ORDER = (
     [("q", 0), ("k", 0), ("k", 1), ("q", 1), ("q", 2), ("k", 2)]
@@ -59,9 +60,13 @@ def tile_normlocalattention_pa_kernel(tc, q_scaled, k_heads, v_heads, out):
     woven_in = {first_group[s]: (s + AHEAD, all_planes) for s in range(1, len(units) - AHEAD)}
     woven_in[0] = (1, all_planes[:PACK])
     woven_in[1] = (2, all_planes)
-    v_pieces = [(h, c) for h in range(1, HEADS) for c in range(N_CHUNKS)]
-    sums_steps = [g for g in range(len(groups) - 1) if g - 2 in unit_ending_at]
-    piece_at = {sums_steps[n + V_LAG]: n for n in range(len(v_pieces))}
+    mx_at = {
+        end + MX_LAG + (s in (0, len(units) - 3)): s
+        for end, s in unit_ending_at.items()
+        if s < len(units) - 2
+    }
+    v_pieces = [(h, c) for h in range(HEADS) for c in range(N_CHUNKS)]
+    piece_at = dict(zip(FIRST_V_STEPS + sorted(mx_at), range(len(v_pieces))))
 
     with ExitStack() as ctx:
         const = ctx.enter_context(tc.tile_pool(name="const", bufs=1))
@@ -80,7 +85,6 @@ def tile_normlocalattention_pa_kernel(tc, q_scaled, k_heads, v_heads, out):
         raw = {}
         flipped = {}
         qk_t = {}
-        v_grouped = {}
         v_piece = {}
         v_words = {}
         v_scales = {}
@@ -119,20 +123,6 @@ def tile_normlocalattention_pa_kernel(tc, q_scaled, k_heads, v_heads, out):
             run = slice(planes[0], planes[-1] + 1)
             nc.vector.tensor_copy(out=qk_t[s][:, run], in_=flipped[s][:, run])
 
-        def group_v(h):
-            v_grouped[h] = v_pool.tile(
-                [P, N_CHUNKS, DH, PACK], BF16, name="v_grouped", align_bytes=64
-            )
-            for c in range(N_CHUNKS):
-                nc.gpsimd.tensor_scalar(
-                    out=v_grouped[h][:, c],
-                    in0=raw[h]["v"][:, c].rearrange("p j d -> p d j"),
-                    scalar1=1.0,
-                    scalar2=0.0,
-                    op0=MULT,
-                    op1=ADD,
-                )
-
         def group_v_piece(n):
             h, c = v_pieces[n]
             v_piece[n] = piece_pool.tile([P, DH, PACK], BF16, name="v_piece", align_bytes=64)
@@ -154,17 +144,6 @@ def tile_normlocalattention_pa_kernel(tc, q_scaled, k_heads, v_heads, out):
                 out=v_words[h][:, c].bitcast(FP8X4),
                 scales=v_scales[h][:, c],
                 in_=v_piece[n][:].rearrange("p d j -> p (d j)"),
-            )
-
-        def quantise_v(h, chunks):
-            if chunks[0] == 0:
-                v_words[h] = v_pool.tile([P, N_CHUNKS, DH], U32, name="v_words", align_bytes=64)
-                v_scales[h] = v_pool.tile([P, N_CHUNKS, DH], U8, name="v_scales", align_bytes=64)
-            run = slice(chunks[0], chunks[-1] + 1)
-            nc.vector.quantize_mx(
-                out=v_words[h][:, run].rearrange("p c d -> p (c d)").bitcast(FP8X4),
-                scales=v_scales[h][:, run].rearrange("p c d -> p (c d)"),
-                in_=v_grouped[h][:, run].rearrange("p c d j -> p (c d j)"),
             )
 
         def first_matmuls(g):
@@ -277,9 +256,7 @@ def tile_normlocalattention_pa_kernel(tc, q_scaled, k_heads, v_heads, out):
                 nc.scalar.copy(out=planes, in_=early[s, first][:])
             else:
                 nc.vector.tensor_copy(out=planes, in_=early[s, first][:])
-        group_v(0)
         group_v_piece(0)
-        first_mx_step = min(unit_ending_at) + 2
 
         last = len(groups) - 1
         for g in range(last):
@@ -298,12 +275,8 @@ def tile_normlocalattention_pa_kernel(tc, q_scaled, k_heads, v_heads, out):
                     group_v_piece(piece_at[g] + 1)
             if g in woven_in:
                 copy_transposes_out(woven_in[g][0], woven_in[g][1])
-            if g == first_mx_step - 1:
-                quantise_v(0, [0, 1])
-            if g == first_group[1] + 2:
-                quantise_v(0, [2, 3])
-            if g - 2 in unit_ending_at:
-                whole_unit(unit_ending_at[g - 2], nc.vector.tensor_copy)
+            if g in mx_at:
+                whole_unit(mx_at[g], nc.vector.tensor_copy)
 
         first_matmuls(last)
         relu_out_of_psum(last, (VECTOR_Q_TILE,))

@@ -23,19 +23,19 @@ Q_TILES = CHUNK // P
 
 AHEAD = 2
 VECTOR_Q_TILE = 1
-SPARE_Q_TILE = 3
+SECOND_Q_TILE = 3
 
-FIRST_V_STEPS = [1, 2]
+FIRST_CHUNKS = 2
 MX_LAG = 2
 
 LOAD_ORDER = (
-    [("q", 0), ("k", 0), ("k", 1), ("q", 1), ("q", 2), ("k", 2)]
+    [("k", 0), ("q", 0), ("k", 1), ("q", 1), ("q", 2), ("k", 2)]
     + [("v", c) for c in range(N_CHUNKS)]
     + [("q", 3), ("k", 3)]
 )
 WARM_UP = 16
 
-BORROWING_GROUP = 1
+BORROWING_GROUP = 0
 
 DOTS_BANKS = 6
 
@@ -58,15 +58,15 @@ def tile_normlocalattention_pa_kernel(tc, q_scaled, k_heads, v_heads, out):
     unit_ending_at = {first_group[s] + len(seen_chunks(w)) - 1: s for s, (h, w) in enumerate(units)}
     all_planes = list(range(2 * PACK))
     woven_in = {first_group[s]: (s + AHEAD, all_planes) for s in range(1, len(units) - AHEAD)}
-    woven_in[0] = (1, all_planes[:PACK])
-    woven_in[1] = (2, all_planes)
+    woven_in[0] = (2, all_planes)
     mx_at = {
         end + MX_LAG + (s in (0, len(units) - 3)): s
         for end, s in unit_ending_at.items()
         if s < len(units) - 2
     }
-    v_pieces = [(h, c) for h in range(HEADS) for c in range(N_CHUNKS)]
-    piece_at = dict(zip(FIRST_V_STEPS + sorted(mx_at), range(len(v_pieces))))
+    two_bank_steps = {0, first_group[-1]}
+    v_pieces = [(h, c) for h in range(HEADS) for c in range(N_CHUNKS)][FIRST_CHUNKS:]
+    piece_at = dict(zip(sorted(mx_at), range(len(v_pieces))))
 
     with ExitStack() as ctx:
         const = ctx.enter_context(tc.tile_pool(name="const", bufs=1))
@@ -93,6 +93,8 @@ def tile_normlocalattention_pa_kernel(tc, q_scaled, k_heads, v_heads, out):
         attn_words = {}
         attn_scales = {}
 
+        zeros = const.tile([P, P], BF16, name="zeros")
+        nc.gpsimd.memset(zeros[:], 0.0)
         identity = const.tile([P, P], BF16, name="identity")
         masks.make_identity(nc, identity[:])
 
@@ -123,17 +125,34 @@ def tile_normlocalattention_pa_kernel(tc, q_scaled, k_heads, v_heads, out):
             run = slice(planes[0], planes[-1] + 1)
             nc.vector.tensor_copy(out=qk_t[s][:, run], in_=flipped[s][:, run])
 
-        def group_v_piece(n):
-            h, c = v_pieces[n]
-            v_piece[n] = piece_pool.tile([P, DH, PACK], BF16, name="v_piece", align_bytes=64)
+        def regroup(out, h, c):
             nc.gpsimd.tensor_scalar(
-                out=v_piece[n][:],
+                out=out,
                 in0=raw[h]["v"][:, c].rearrange("p j d -> p d j"),
                 scalar1=1.0,
                 scalar2=0.0,
                 op0=MULT,
                 op1=ADD,
             )
+
+        def regroup_first_chunks():
+            first_v = const.tile([P, FIRST_CHUNKS, DH, PACK], BF16, name="first_v", align_bytes=64)
+            for c in range(FIRST_CHUNKS):
+                regroup(first_v[:, c], 0, c)
+            return first_v
+
+        def quantise_first_chunks(first_v):
+            v_words[0] = v_pool.tile([P, N_CHUNKS, DH], U32, name="v_words", align_bytes=64)
+            v_scales[0] = v_pool.tile([P, N_CHUNKS, DH], U8, name="v_scales", align_bytes=64)
+            nc.vector.quantize_mx(
+                out=v_words[0][:, :FIRST_CHUNKS].rearrange("p c d -> p (c d)").bitcast(FP8X4),
+                scales=v_scales[0][:, :FIRST_CHUNKS].rearrange("p c d -> p (c d)"),
+                in_=first_v[:].rearrange("p c d j -> p (c d j)"),
+            )
+
+        def regroup_piece(n):
+            v_piece[n] = piece_pool.tile([P, DH, PACK], BF16, name="v_piece", align_bytes=64)
+            regroup(v_piece[n][:], *v_pieces[n])
 
         def quantise_v_piece(n):
             h, c = v_pieces[n]
@@ -230,15 +249,13 @@ def tile_normlocalattention_pa_kernel(tc, q_scaled, k_heads, v_heads, out):
 
         load_head(0)
         load_head(1)
-        zeros = const.tile([P, P], BF16, name="zeros")
-        nc.vector.memset(zeros[:], 0.0)
         unread = dots_pool.tile([P, PACK, P], F32, name="dots")
         for i in range(WARM_UP):
             nc.tensor.matmul(
                 out=unread[:, i % PACK, :], lhsT=zeros[:], rhs=zeros[:], start=True, stop=True
             )
         early = {}
-        halves = [(0, PACK), (0, 0), (1, PACK)]
+        halves = [(0, PACK), (0, 0), (1, PACK), (1, 0)]
         for s, first in halves:
             early[s, first] = dots_pool.tile([P, PACK, P], BF16, name="dots")
             h, c = units[s]
@@ -254,9 +271,13 @@ def tile_normlocalattention_pa_kernel(tc, q_scaled, k_heads, v_heads, out):
             planes = qk_t[s][:, first : first + PACK, :]
             if first:
                 nc.scalar.copy(out=planes, in_=early[s, first][:])
-            else:
+            elif s:
                 nc.vector.tensor_copy(out=planes, in_=early[s, first][:])
-        group_v_piece(0)
+            else:
+                nc.vector.tensor_copy(out=planes[:, :1], in_=early[s, first][:, :1])
+                nc.vector.tensor_copy(out=planes[:, 1:], in_=early[s, first][:, 1:])
+        first_v = regroup_first_chunks()
+        regroup_piece(0)
 
         last = len(groups) - 1
         for g in range(last):
@@ -265,16 +286,19 @@ def tile_normlocalattention_pa_kernel(tc, q_scaled, k_heads, v_heads, out):
             if g == first_group[s] and w == 0 and h + 2 < HEADS:
                 load_head(h + 2)
             first_matmuls(g)
-            spare = g == first_group[s] and g not in woven_in
-            relu_out_of_psum(g, (VECTOR_Q_TILE, SPARE_Q_TILE) if spare else (VECTOR_Q_TILE,))
+            relu_out_of_psum(
+                g, (VECTOR_Q_TILE, SECOND_Q_TILE) if g in two_bank_steps else (VECTOR_Q_TILE,)
+            )
             if g >= 1:
                 quantise_attn(g - 1, 1)
             if g in piece_at:
                 quantise_v_piece(piece_at[g])
                 if piece_at[g] + 1 < len(v_pieces):
-                    group_v_piece(piece_at[g] + 1)
+                    regroup_piece(piece_at[g] + 1)
             if g in woven_in:
                 copy_transposes_out(woven_in[g][0], woven_in[g][1])
+            if g == min(mx_at) - 1:
+                quantise_first_chunks(first_v)
             if g in mx_at:
                 whole_unit(mx_at[g], nc.vector.tensor_copy)
 

@@ -35,9 +35,8 @@ LOAD_ORDER = (
 )
 WARM_UP = 16
 
-BORROWING_GROUP = 0
-
-DOTS_BANKS = 6
+TRANSPOSES_FROM = 2
+PSUM_BANKS = 8
 
 FLOPS = 2 * 2 * HEADS * 10 * CHUNK * CHUNK * DH
 
@@ -60,9 +59,7 @@ def tile_normlocalattention_pa_kernel(tc, q_scaled, k_heads, v_heads, out):
     woven_in = {first_group[s]: (s + AHEAD, all_planes) for s in range(1, len(units) - AHEAD)}
     woven_in[0] = (2, all_planes)
     mx_at = {
-        end + MX_LAG + (s in (0, len(units) - 3)): s
-        for end, s in unit_ending_at.items()
-        if s < len(units) - 2
+        end + MX_LAG + (s == 0): s for end, s in unit_ending_at.items() if s < len(units) - 2
     }
     two_bank_steps = {0, first_group[-1]}
     v_pieces = [(h, c) for h in range(HEADS) for c in range(N_CHUNKS)][FIRST_CHUNKS:]
@@ -77,9 +74,7 @@ def tile_normlocalattention_pa_kernel(tc, q_scaled, k_heads, v_heads, out):
         stage = ctx.enter_context(tc.tile_pool(name="stage", bufs=5))
         result_pool = ctx.enter_context(tc.tile_pool(name="result", bufs=5))
         attn_pool = ctx.enter_context(tc.tile_pool(name="attn", bufs=9))
-        dots_pool = ctx.enter_context(tc.psum_pool(name="dots", bufs=DOTS_BANKS))
-        flip_pool = ctx.enter_context(tc.psum_pool(name="flip", bufs=1))
-        sums_pool = ctx.enter_context(tc.psum_pool(name="sums", bufs=1))
+        bank_pool = ctx.enter_context(tc.psum_pool(name="banks", bufs=PSUM_BANKS))
         ctx.enter_context(tc.manual_schedule())
 
         raw = {}
@@ -170,15 +165,15 @@ def tile_normlocalattention_pa_kernel(tc, q_scaled, k_heads, v_heads, out):
             h, w = units[s]
             keys = qk_t[h * N_CHUNKS + c]
             ahead, planes = woven_in.get(g, (None, []))
-            if planes and g == BORROWING_GROUP:
-                flipped[ahead] = sums_pool.tile([P, 2 * PACK, P], BF16, name="borrowed", tag="sums")
-            elif planes:
-                flipped[ahead] = flip_pool.tile([P, 2 * PACK, P], BF16, name="flipped")
-            places = 2 * Q_TILES
             banks[g] = []
             for t in range(Q_TILES):
-                bank = dots_pool.tile([P, PACK, P], F32, name="dots")
+                if planes and t == TRANSPOSES_FROM:
+                    flipped[ahead] = bank_pool.tile([P, 2 * PACK, P], BF16, name="bank")
+                bank = bank_pool.tile([P, PACK, P], F32, name="bank")
                 for j in range(PACK):
+                    n = (t - TRANSPOSES_FROM) * PACK + j
+                    if planes and 0 <= n < len(planes):
+                        transpose_plane(ahead, planes[n])
                     nc.tensor.matmul(
                         out=bank[:, j, :],
                         lhsT=keys[:, PACK + j, :],
@@ -186,9 +181,6 @@ def tile_normlocalattention_pa_kernel(tc, q_scaled, k_heads, v_heads, out):
                         start=True,
                         stop=True,
                     )
-                    place = 2 * t + j // 2
-                    if j % 2 == 0 and place >= places - len(planes):
-                        transpose_plane(ahead, planes[place - (places - len(planes))])
                 banks[g].append(bank)
 
         def relu_out_of_psum(g, vector_tiles):
@@ -244,12 +236,12 @@ def tile_normlocalattention_pa_kernel(tc, q_scaled, k_heads, v_heads, out):
             )
 
         def whole_unit(s, copy_out):
-            sums = sums_pool.tile([P, Q_TILES, DH], F32, name="sums", tag="sums")
+            sums = bank_pool.tile([P, Q_TILES, DH], F32, name="bank")
             second_matmuls(s, list(range(Q_TILES)), sums, copy_out)
 
         load_head(0)
         load_head(1)
-        unread = dots_pool.tile([P, PACK, P], F32, name="dots")
+        unread = bank_pool.tile([P, PACK, P], F32, name="bank")
         for i in range(WARM_UP):
             nc.tensor.matmul(
                 out=unread[:, i % PACK, :], lhsT=zeros[:], rhs=zeros[:], start=True, stop=True
@@ -257,7 +249,7 @@ def tile_normlocalattention_pa_kernel(tc, q_scaled, k_heads, v_heads, out):
         early = {}
         halves = [(0, PACK), (0, 0), (1, PACK), (1, 0)]
         for s, first in halves:
-            early[s, first] = dots_pool.tile([P, PACK, P], BF16, name="dots")
+            early[s, first] = bank_pool.tile([P, PACK, P], BF16, name="bank")
             h, c = units[s]
             for j in range(PACK):
                 nc.tensor.transpose(
@@ -308,5 +300,5 @@ def tile_normlocalattention_pa_kernel(tc, q_scaled, k_heads, v_heads, out):
         whole_unit(unit_ending_at[last - 2], nc.scalar.copy)
         quantise_attn(last, Q_TILES)
         for t in range(Q_TILES):
-            tile_sums = dots_pool.tile([P, 1, DH], F32, name="dots")
+            tile_sums = bank_pool.tile([P, 1, DH], F32, name="bank")
             second_matmuls(len(units) - 1, [t], tile_sums, nc.vector.tensor_copy)

@@ -35,8 +35,7 @@ LOAD_ORDER = (
 )
 WARM_UP = 16
 
-TRANSPOSES_FROM = 2
-PSUM_BANKS = 8
+RING_BANKS = 7
 
 FLOPS = 2 * 2 * HEADS * 10 * CHUNK * CHUNK * DH
 
@@ -74,7 +73,8 @@ def tile_normlocalattention_pa_kernel(tc, q_scaled, k_heads, v_heads, out):
         stage = ctx.enter_context(tc.tile_pool(name="stage", bufs=5))
         result_pool = ctx.enter_context(tc.tile_pool(name="result", bufs=5))
         attn_pool = ctx.enter_context(tc.tile_pool(name="attn", bufs=9))
-        bank_pool = ctx.enter_context(tc.psum_pool(name="banks", bufs=PSUM_BANKS))
+        flip_pool = ctx.enter_context(tc.psum_pool(name="flip", bufs=1))
+        bank_pool = ctx.enter_context(tc.psum_pool(name="banks", bufs=RING_BANKS))
         ctx.enter_context(tc.manual_schedule())
 
         raw = {}
@@ -165,15 +165,12 @@ def tile_normlocalattention_pa_kernel(tc, q_scaled, k_heads, v_heads, out):
             h, w = units[s]
             keys = qk_t[h * N_CHUNKS + c]
             ahead, planes = woven_in.get(g, (None, []))
+            if planes:
+                flipped[ahead] = flip_pool.tile([P, 2 * PACK, P], BF16, name="flipped")
             banks[g] = []
             for t in range(Q_TILES):
-                if planes and t == TRANSPOSES_FROM:
-                    flipped[ahead] = bank_pool.tile([P, 2 * PACK, P], BF16, name="bank")
                 bank = bank_pool.tile([P, PACK, P], F32, name="bank")
                 for j in range(PACK):
-                    n = (t - TRANSPOSES_FROM) * PACK + j
-                    if planes and 0 <= n < len(planes):
-                        transpose_plane(ahead, planes[n])
                     nc.tensor.matmul(
                         out=bank[:, j, :],
                         lhsT=keys[:, PACK + j, :],
@@ -181,6 +178,8 @@ def tile_normlocalattention_pa_kernel(tc, q_scaled, k_heads, v_heads, out):
                         start=True,
                         stop=True,
                     )
+                    if planes and j % 2 == 0:
+                        transpose_plane(ahead, planes[2 * t + j // 2])
                 banks[g].append(bank)
 
         def relu_out_of_psum(g, vector_tiles):

@@ -33,7 +33,7 @@ LOAD_ORDER = (
     + [("v", c) for c in range(N_CHUNKS)]
     + [("q", 3), ("k", 3)]
 )
-WARM_UP = 16
+WARM_UP = 12
 
 RING_BANKS = 7
 

from contextlib import ExitStack

import concourse.masks as masks
import concourse.mybir as mybir

BF16 = mybir.dt.bfloat16
F32 = mybir.dt.float32
U32 = mybir.dt.uint32
U8 = mybir.dt.uint8
FP8X4 = mybir.dt.float8_e4m3fn_x4
RELU = mybir.ActivationFunctionType.Relu
MULT = mybir.AluOpType.mult
ADD = mybir.AluOpType.add

HEADS = 8
TOKENS = 2048
DH = 128
P = 128
PACK = 4
CHUNK = P * PACK
N_CHUNKS = TOKENS // CHUNK
Q_TILES = CHUNK // P

AHEAD = 2
VECTOR_Q_TILE = 1
SECOND_Q_TILE = 3

FIRST_CHUNKS = 2
MX_LAG = 2

LOAD_ORDER = (
    [("k", 0), ("q", 0), ("k", 1), ("q", 1), ("q", 2), ("k", 2)]
    + [("v", c) for c in range(N_CHUNKS)]
    + [("q", 3), ("k", 3)]
)
WARM_UP = 12

RING_BANKS = 7

FLOPS = 2 * 2 * HEADS * 10 * CHUNK * CHUNK * DH


def seen_chunks(w):
    return list(range(max(w - 1, 0), min(w + 2, N_CHUNKS)))


def tile_normlocalattention_pa_kernel(tc, q_scaled, k_heads, v_heads, out):
    nc = tc.nc

    units = [(h, w) for h in range(HEADS) for w in range(N_CHUNKS)]
    groups = []
    first_group = []
    for s, (h, w) in enumerate(units):
        first_group.append(len(groups))
        groups.extend((s, c) for c in seen_chunks(w))
    unit_ending_at = {first_group[s] + len(seen_chunks(w)) - 1: s for s, (h, w) in enumerate(units)}
    all_planes = list(range(2 * PACK))
    woven_in = {first_group[s]: (s + AHEAD, all_planes) for s in range(1, len(units) - AHEAD)}
    woven_in[0] = (2, all_planes)
    mx_at = {
        end + MX_LAG + (s == 0): s for end, s in unit_ending_at.items() if s < len(units) - 2
    }
    two_bank_steps = {0, first_group[-1]}
    v_pieces = [(h, c) for h in range(HEADS) for c in range(N_CHUNKS)][FIRST_CHUNKS:]
    piece_at = dict(zip(sorted(mx_at), range(len(v_pieces))))

    with ExitStack() as ctx:
        const = ctx.enter_context(tc.tile_pool(name="const", bufs=1))
        raw_pool = ctx.enter_context(tc.tile_pool(name="raw", bufs=3))
        qk_pool = ctx.enter_context(tc.tile_pool(name="qk", bufs=AHEAD + 3))
        v_pool = ctx.enter_context(tc.tile_pool(name="v", bufs=2))
        piece_pool = ctx.enter_context(tc.tile_pool(name="piece", bufs=1))
        stage = ctx.enter_context(tc.tile_pool(name="stage", bufs=5))
        result_pool = ctx.enter_context(tc.tile_pool(name="result", bufs=5))
        attn_pool = ctx.enter_context(tc.tile_pool(name="attn", bufs=9))
        flip_pool = ctx.enter_context(tc.psum_pool(name="flip", bufs=1))
        bank_pool = ctx.enter_context(tc.psum_pool(name="banks", bufs=RING_BANKS))
        ctx.enter_context(tc.manual_schedule())

        raw = {}
        flipped = {}
        qk_t = {}
        v_piece = {}
        v_words = {}
        v_scales = {}
        banks = {}
        attn_grouped = {}
        attn_words = {}
        attn_scales = {}

        zeros = const.tile([P, P], BF16, name="zeros")
        nc.gpsimd.memset(zeros[:], 0.0)
        identity = const.tile([P, P], BF16, name="identity")
        masks.make_identity(nc, identity[:])

        def load_head(h):
            raw[h] = {
                "q": raw_pool.tile([P, N_CHUNKS, PACK, DH], BF16, name="q_raw", tag="q_raw"),
                "k": raw_pool.tile([P, N_CHUNKS, PACK, DH], BF16, name="k_raw", tag="k_raw"),
                "v": raw_pool.tile([P, N_CHUNKS, PACK, DH], BF16, name="v_raw", tag="v_raw"),
            }
            sources = {"q": q_scaled, "k": k_heads, "v": v_heads}
            for name, c in LOAD_ORDER:
                rows = slice(c * CHUNK, (c + 1) * CHUNK)
                nc.sync.dma_start(
                    out=raw[h][name][:, c],
                    in_=sources[name][h, rows, :].rearrange("(p j) d -> p j d", j=PACK),
                )

        def transpose_plane(s, plane):
            h, c = units[s]
            source = raw[h]["q" if plane < PACK else "k"]
            nc.tensor.transpose(
                out=flipped[s][:, plane, :], in_=source[:, c, plane % PACK, :], identity=identity[:]
            )

        def copy_transposes_out(s, planes):
            if s not in qk_t:
                qk_t[s] = qk_pool.tile([P, 2 * PACK, P], BF16, name="qk_t")
            run = slice(planes[0], planes[-1] + 1)
            nc.vector.tensor_copy(out=qk_t[s][:, run], in_=flipped[s][:, run])

        def regroup(out, h, c):
            nc.gpsimd.tensor_scalar(
                out=out,
                in0=raw[h]["v"][:, c].rearrange("p j d -> p d j"),
                scalar1=1.0,
                scalar2=0.0,
                op0=MULT,
                op1=ADD,
            )

        def regroup_first_chunks():
            first_v = const.tile([P, FIRST_CHUNKS, DH, PACK], BF16, name="first_v", align_bytes=64)
            for c in range(FIRST_CHUNKS):
                regroup(first_v[:, c], 0, c)
            return first_v

        def quantise_first_chunks(first_v):
            v_words[0] = v_pool.tile([P, N_CHUNKS, DH], U32, name="v_words", align_bytes=64)
            v_scales[0] = v_pool.tile([P, N_CHUNKS, DH], U8, name="v_scales", align_bytes=64)
            nc.vector.quantize_mx(
                out=v_words[0][:, :FIRST_CHUNKS].rearrange("p c d -> p (c d)").bitcast(FP8X4),
                scales=v_scales[0][:, :FIRST_CHUNKS].rearrange("p c d -> p (c d)"),
                in_=first_v[:].rearrange("p c d j -> p (c d j)"),
            )

        def regroup_piece(n):
            v_piece[n] = piece_pool.tile([P, DH, PACK], BF16, name="v_piece", align_bytes=64)
            regroup(v_piece[n][:], *v_pieces[n])

        def quantise_v_piece(n):
            h, c = v_pieces[n]
            if c == 0:
                v_words[h] = v_pool.tile([P, N_CHUNKS, DH], U32, name="v_words", align_bytes=64)
                v_scales[h] = v_pool.tile([P, N_CHUNKS, DH], U8, name="v_scales", align_bytes=64)
            nc.vector.quantize_mx(
                out=v_words[h][:, c].bitcast(FP8X4),
                scales=v_scales[h][:, c],
                in_=v_piece[n][:].rearrange("p d j -> p (d j)"),
            )

        def first_matmuls(g):
            s, c = groups[g]
            h, w = units[s]
            keys = qk_t[h * N_CHUNKS + c]
            ahead, planes = woven_in.get(g, (None, []))
            if planes:
                flipped[ahead] = flip_pool.tile([P, 2 * PACK, P], BF16, name="flipped")
            banks[g] = []
            for t in range(Q_TILES):
                bank = bank_pool.tile([P, PACK, P], F32, name="bank")
                for j in range(PACK):
                    nc.tensor.matmul(
                        out=bank[:, j, :],
                        lhsT=keys[:, PACK + j, :],
                        rhs=qk_t[s][:, t, :],
                        start=True,
                        stop=True,
                    )
                    if planes and j % 2 == 0:
                        transpose_plane(ahead, planes[2 * t + j // 2])
                banks[g].append(bank)

        def relu_out_of_psum(g, vector_tiles):
            attn_grouped[g] = stage.tile(
                [P, Q_TILES, P, PACK], BF16, name="attn_grouped", align_bytes=64
            )
            for t in range(Q_TILES):
                by_query = banks[g][t][:].rearrange("p j q -> p q j")
                if t in vector_tiles:
                    nc.vector.tensor_scalar_max(
                        out=attn_grouped[g][:, t], in0=by_query, scalar1=0.0
                    )
                else:
                    nc.scalar.activation(out=attn_grouped[g][:, t], in_=by_query, func=RELU)

        def quantise_attn(g, pieces):
            attn_words[g] = attn_pool.tile([P, CHUNK], U32, name="attn_words", align_bytes=64)
            attn_scales[g] = attn_pool.tile([P, CHUNK], U8, name="attn_scales", align_bytes=64)
            width = CHUNK // pieces
            for n in range(pieces):
                nc.vector.quantize_mx(
                    out=attn_words[g][:, n * width : (n + 1) * width].bitcast(FP8X4),
                    scales=attn_scales[g][:, n * width : (n + 1) * width],
                    in_=attn_grouped[g][:].rearrange("p t q j -> p (t q j)")[
                        :, n * width * PACK : (n + 1) * width * PACK
                    ],
                )

        def second_matmuls(s, tiles, sums, copy_out):
            h, w = units[s]
            chunks = seen_chunks(w)
            for n, t in enumerate(tiles):
                queries = slice(t * P, (t + 1) * P)
                for i, c in enumerate(chunks):
                    g = first_group[s] + i
                    nc.tensor.matmul_mx(
                        out=sums[:, n, :],
                        lhsT=attn_words[g][:, queries].bitcast(FP8X4),
                        lhsT_scale=attn_scales[g][:, queries],
                        rhs=v_words[h][:, c, :].bitcast(FP8X4),
                        rhs_scale=v_scales[h][:, c, :],
                        start=(i == 0),
                        stop=(i == len(chunks) - 1),
                    )
            result = result_pool.tile([P, len(tiles), DH], F32, name="result")
            copy_out(out=result[:], in_=sums[:])
            rows = slice(w * CHUNK, (w + 1) * CHUNK)
            nc.sync.dma_start(
                out=out[h, rows, :].rearrange("(p t) d -> p t d", t=Q_TILES)[
                    :, tiles[0] : tiles[-1] + 1, :
                ],
                in_=result[:],
            )

        def whole_unit(s, copy_out):
            sums = bank_pool.tile([P, Q_TILES, DH], F32, name="bank")
            second_matmuls(s, list(range(Q_TILES)), sums, copy_out)

        load_head(0)
        load_head(1)
        unread = bank_pool.tile([P, PACK, P], F32, name="bank")
        for i in range(WARM_UP):
            nc.tensor.matmul(
                out=unread[:, i % PACK, :], lhsT=zeros[:], rhs=zeros[:], start=True, stop=True
            )
        early = {}
        halves = [(0, PACK), (0, 0), (1, PACK), (1, 0)]
        for s, first in halves:
            early[s, first] = bank_pool.tile([P, PACK, P], BF16, name="bank")
            h, c = units[s]
            for j in range(PACK):
                nc.tensor.transpose(
                    out=early[s, first][:, j, :],
                    in_=raw[h]["k" if first else "q"][:, c, j, :],
                    identity=identity[:],
                )
        for s in range(AHEAD):
            qk_t[s] = qk_pool.tile([P, 2 * PACK, P], BF16, name="qk_t")
        for s, first in halves:
            planes = qk_t[s][:, first : first + PACK, :]
            if first:
                nc.scalar.copy(out=planes, in_=early[s, first][:])
            elif s:
                nc.vector.tensor_copy(out=planes, in_=early[s, first][:])
            else:
                nc.vector.tensor_copy(out=planes[:, :1], in_=early[s, first][:, :1])
                nc.vector.tensor_copy(out=planes[:, 1:], in_=early[s, first][:, 1:])
        first_v = regroup_first_chunks()
        regroup_piece(0)

        last = len(groups) - 1
        for g in range(last):
            s, c = groups[g]
            h, w = units[s]
            if g == first_group[s] and w == 0 and h + 2 < HEADS:
                load_head(h + 2)
            first_matmuls(g)
            relu_out_of_psum(
                g, (VECTOR_Q_TILE, SECOND_Q_TILE) if g in two_bank_steps else (VECTOR_Q_TILE,)
            )
            if g >= 1:
                quantise_attn(g - 1, 1)
            if g in piece_at:
                quantise_v_piece(piece_at[g])
                if piece_at[g] + 1 < len(v_pieces):
                    regroup_piece(piece_at[g] + 1)
            if g in woven_in:
                copy_transposes_out(woven_in[g][0], woven_in[g][1])
            if g == min(mx_at) - 1:
                quantise_first_chunks(first_v)
            if g in mx_at:
                whole_unit(mx_at[g], nc.vector.tensor_copy)

        first_matmuls(last)
        relu_out_of_psum(last, (VECTOR_Q_TILE,))
        quantise_attn(last - 1, 1)
        whole_unit(unit_ending_at[last - 2], nc.scalar.copy)
        quantise_attn(last, Q_TILES)
        for t in range(Q_TILES):
            tile_sums = bank_pool.tile([P, 1, DH], F32, name="bank")
            second_matmuls(len(units) - 1, [t], tile_sums, nc.vector.tensor_copy)
